import numpy as np
import ml_dtypes


def mxq(x, axis, fmt="e4m3"):
    dtype, down = {"e4m3": (ml_dtypes.float8_e4m3fn, 7), "e5m2": (ml_dtypes.float8_e5m2, 14)}[fmt]
    v = np.moveaxis(np.asarray(x, np.float32).astype(ml_dtypes.bfloat16).astype(np.float64), axis, -1)
    blocks = v.reshape(v.shape[:-1] + (-1, 32))
    amax = np.abs(blocks).max(-1, keepdims=True)
    byte = np.maximum(np.where(amax > 0, np.frexp(amax)[1] - 1 + 127, 0) - down, 1)
    scale = np.exp2(byte - 127.0)
    codes = (blocks / scale).astype(np.float32).astype(dtype).astype(np.float64)
    return np.moveaxis((codes * scale).reshape(v.shape), -1, axis)


WIDE = False


def mx_kscale(k):
    if not WIDE:
        return np.ones(k)
    levels = np.array([10, -10, 5, -5, 0])
    a = np.random.permutation(np.resize(levels, k // 512 * 4)).reshape(k // 512, 4)
    idx = np.arange(k)
    return np.exp2(a[idx // 512, idx % 128 // 32])


BF16 = ml_dtypes.bfloat16


def bf(x):
    return np.asarray(x, np.float32).astype(BF16)


def f64(x):
    return np.asarray(x).astype(np.float64)


E, T, D, H = 2, 256, 2048, 1024


def silu(v):
    return v / (1.0 + np.exp(-v))


def setup_inputs():
    s, t = mx_kscale(D), mx_kscale(H)
    x = np.random.standard_normal((E * T, D)) * s
    w13 = np.random.standard_normal((E, 2 * H, D)) * 0.022 / s[None, None, :]
    w13[:, H:, :] = w13[:, H:, :] * t[None, :, None]
    w2 = np.random.standard_normal((E, D, H)) * 0.04 / t[None, None, :]
    return {"x": bf(x), "w13": bf(w13), "w2": bf(w2),
            "num_tokens_per_expert": np.full((E,), T, dtype=np.int32)}


def reference(x, w13, w2, num_tokens_per_expert):
    xg = f64(x).reshape(E, T, D)
    h13 = mxq(xg, 2, "e4m3") @ mxq(f64(w13), 2, "e4m3").transpose(0, 2, 1)
    h1, h3 = h13[..., :H], h13[..., H:]
    h = silu(h1) * h3
    out = mxq(h, 2, "e4m3") @ mxq(f64(w2), 2, "e4m3").transpose(0, 2, 1)
    return out.reshape(E * T, D)

@@ -1,0 +1,223 @@
+from contextlib import ExitStack
+
+import concourse.mybir as mybir
+from concourse.masks import make_identity
+
+FP8X4 = mybir.dt.float8_e4m3fn_x4
+BF16 = mybir.dt.bfloat16
+F32 = mybir.dt.float32
+U32 = mybir.dt.uint32
+U8 = mybir.dt.uint8
+SILU = mybir.ActivationFunctionType.Silu
+MULT = mybir.AluOpType.mult
+
+E = 2
+T = 256
+D = 2048
+H = 1024
+P = 128
+FLOPS = 2 * E * T * (D * 2 * H + H * D)
+
+RAW_BUFS = 10
+LOOKAHEAD = 8
+
+
+def tile_synclessmxfp8moe_kernel(tc, x, w13, w2, num_tokens_per_expert, out):
+    nc = tc.nc
+    with ExitStack() as ctx:
+        const = ctx.enter_context(tc.tile_pool(name="const", bufs=1))
+        rawp = ctx.enter_context(tc.tile_pool(name="rawp", bufs=RAW_BUFS))
+        grpp = ctx.enter_context(tc.tile_pool(name="grpp", bufs=3))
+        codp = ctx.enter_context(tc.tile_pool(name="codp", bufs=6))
+        keep = ctx.enter_context(tc.tile_pool(name="keep", bufs=2))
+        silp = ctx.enter_context(tc.tile_pool(name="silp", bufs=2))
+        outp = ctx.enter_context(tc.tile_pool(name="outp", bufs=4))
+        tps = ctx.enter_context(tc.psum_pool(name="tps", bufs=6))
+        mps = ctx.enter_context(tc.psum_pool(name="mps", bufs=2))
+        ctx.enter_context(tc.manual_schedule())
+
+        blocks = [("x", 0, 0, 0)]
+        for e in range(E):
+            for b in range(4):
+                blocks.append(("w13", e, 0, b))
+                blocks.append(("w13", e, 1, b))
+            if e == 0:
+                blocks.append(("x", 1, 0, 0))
+            for c in range(4):
+                blocks.append(("w2", e, 0, c))
+        index = dict((blk, n) for n, blk in enumerate(blocks))
+
+        raw = {}
+        codes = {}
+        hstate = {}
+
+        def load(n):
+            kind, e, hf, b = blocks[n]
+            r = rawp.tile([P, 4096], BF16, tag="raw", name="raw")
+            if kind == "x":
+                src = x[T * e : T * (e + 1), :].rearrange("(p i) d -> p i d", i=2)
+                dst = r[:].rearrange("p (i d) -> p i d", i=2)
+            elif kind == "w13":
+                r0 = H * hf + 256 * b
+                src = w13[e, r0 : r0 + 256, :].rearrange("(p i) d -> p i d", i=2)
+                dst = r[:].rearrange("p (i d) -> p i d", i=2)
+            else:
+                src = w2[e, 512 * b : 512 * (b + 1), :].rearrange("(p j) h -> p j h", j=4)
+                dst = r[:].rearrange("p (j h) -> p j h", j=4)
+            nc.sync.dma_start(out=dst, in_=src)
+            raw[n] = r
+
+        def copy_on(eng, dst, src):
+            if eng == "S":
+                nc.scalar.copy(out=dst, in_=src)
+            else:
+                nc.vector.tensor_copy(out=dst, in_=src)
+
+        def block(n):
+            kind, e, hf, b = blocks[n]
+            if n + LOOKAHEAD < len(blocks):
+                load(n + LOOKAHEAD)
+            words = raw[n][:].bitcast(F32)
+            banks = []
+            for k in range(4):
+                bank = tps.tile([P, 512], F32, tag="tb", name="tb")
+                for s in range(2):
+                    slot = 2 * k + s
+                    for u in range(2):
+                        if kind == "w2":
+                            beta = 4 * (slot % 4) + 2 * (slot // 4) + u
+                        else:
+                            beta = 8 * (slot % 2) + 2 * (slot // 2) + u
+                        q = 2 * s + u
+                        nc.tensor.transpose(
+                            bank[:, q * P : (q + 1) * P],
+                            words[:, beta * P : (beta + 1) * P],
+                            ident[:],
+                        )
+                banks.append(bank)
+            engines = {"x": "SVSV", "w13": "SSVS", "w2": "SSVV"}[kind]
+            grouped = grpp.tile([P, 4096], BF16, tag="grp", name="grp", align_bytes=64)
+            gw = grouped[:].bitcast(F32)
+            for k in range(4):
+                copy_on(
+                    engines[k],
+                    gw[:, k * 512 : (k + 1) * 512].rearrange("p (s r u) -> p s r u", s=2, u=2),
+                    banks[k][:].rearrange("p (s u r) -> p s r u", s=2, u=2),
+                )
+            if kind == "x":
+                cw = keep.tile([P, 1024], U32, tag="xc", name="xc", align_bytes=64)
+                cs = keep.tile([P, 1024], U8, tag="xs", name="xs", align_bytes=64)
+            else:
+                cw = codp.tile([P, 1024], U32, tag="cw", name="cw", align_bytes=64)
+                cs = codp.tile([P, 1024], U8, tag="cs", name="cs", align_bytes=64)
+            for hlf in range(2):
+                nc.vector.quantize_mx(
+                    out=cw[:, hlf * 512 : (hlf + 1) * 512].bitcast(FP8X4),
+                    scales=cs[:, hlf * 512 : (hlf + 1) * 512],
+                    in_=grouped[:, hlf * 2048 : (hlf + 1) * 2048],
+                )
+            codes[n] = (cw, cs)
+
+        def mm1(e, b):
+            xc, xs = codes[index[("x", e, 0, 0)]]
+            halves = []
+            for hf in range(2):
+                cw, cs = codes[index[("w13", e, hf, b)]]
+                bank = mps.tile([P, 512], F32, tag="mm", name="mm")
+                for ep in range(2):
+                    for g in range(4):
+                        sl = slice((2 * g + ep) * P, (2 * g + ep + 1) * P)
+                        xl = slice(g * 256, (g + 1) * 256)
+                        nc.tensor.matmul_mx(
+                            out=bank[:, ep * 256 : (ep + 1) * 256],
+                            lhsT=cw[:, sl].bitcast(FP8X4),
+                            lhsT_scale=cs[:, sl],
+                            rhs=xc[:, xl].bitcast(FP8X4),
+                            rhs_scale=xs[:, xl],
+                            start=(g == 0),
+                            stop=(g == 3),
+                        )
+                halves.append(bank)
+            sil = silp.tile([P, 512], F32, tag="sil", name="sil")
+            nc.scalar.activation(out=sil[:], in_=halves[0][:], func=SILU)
+            if b == 0:
+                hg = keep.tile([P, 2, 256, 4], BF16, tag="hg", name="hg", align_bytes=64)
+                hc = keep.tile([P, 512], U32, tag="hc", name="hc", align_bytes=64)
+                hs = keep.tile([P, 512], U8, tag="hs", name="hs", align_bytes=64)
+                hstate[e] = (hg, hc, hs)
+            hg, hc, hs = hstate[e]
+            gp, up = b // 2, b % 2
+            nc.vector.tensor_tensor(
+                out=hg[:, gp, :, 2 * up : 2 * up + 2],
+                in0=halves[1][:].rearrange("p (e n) -> p n e", e=2),
+                in1=sil[:].rearrange("p (e n) -> p n e", e=2),
+                op=MULT,
+            )
+            if up == 1:
+                nc.vector.quantize_mx(
+                    out=hc[:, gp * 256 : (gp + 1) * 256].bitcast(FP8X4),
+                    scales=hs[:, gp * 256 : (gp + 1) * 256],
+                    in_=hg[:, gp, :, :].rearrange("p n t -> p (n t)"),
+                )
+
+        def mm2(e, c, engines):
+            cw, cs = codes[index[("w2", e, 0, c)]]
+            hg, hc, hs = hstate[e]
+            o = outp.tile([P, 2, 512], F32, tag="o", name="o")
+            for i in range(2):
+                bank = mps.tile([P, 512], F32, tag="mm", name="mm")
+                for gp in range(2):
+                    hl = slice(gp * 256 + i * P, gp * 256 + (i + 1) * P)
+                    wl = slice(gp * 512, (gp + 1) * 512)
+                    nc.tensor.matmul_mx(
+                        out=bank[:],
+                        lhsT=hc[:, hl].bitcast(FP8X4),
+                        lhsT_scale=hs[:, hl],
+                        rhs=cw[:, wl].bitcast(FP8X4),
+                        rhs_scale=cs[:, wl],
+                        start=(gp == 0),
+                        stop=(gp == 1),
+                    )
+                copy_on(
+                    engines[i],
+                    o[:, i, :].rearrange("p (r j) -> p r j", j=4),
+                    bank[:].rearrange("p (j r) -> p r j", j=4),
+                )
+            nc.sync.dma_start(
+                out=out[T * e : T * (e + 1), 512 * c : 512 * (c + 1)].rearrange(
+                    "(m i) c -> m i c", i=2
+                ),
+                in_=o[:],
+            )
+
+        for n in range(LOOKAHEAD):
+            load(n)
+        ident = const.tile([P, P], F32, name="ident")
+        make_identity(nc, ident[:])
+        warm_in = const.tile([P, 8], F32, name="warm_in")
+        warm_out = const.tile([P, 8], F32, name="warm_out")
+        nc.vector.memset(warm_in[:], 0.0)
+        nc.scalar.activation(out=warm_out[:], in_=warm_in[:], func=SILU)
+
+        after = {
+            3: [("m1", 0, 0)],
+            5: [("m1", 0, 1)],
+            8: [("m1", 0, 2)],
+            10: [("m1", 0, 3)],
+            12: [("m2", 0, 0)],
+            13: [("m2", 0, 1)],
+            14: [("m2", 0, 2)],
+            15: [("m2", 0, 3)],
+            17: [("m1", 1, 0)],
+            19: [("m1", 1, 1)],
+            21: [("m1", 1, 2)],
+            23: [("m1", 1, 3)],
+            25: [("m2", 1, 0), ("m2", 1, 1), ("m2", 1, 2), ("m2", 1, 3)],
+        }
+        for n in range(len(blocks)):
+            block(n)
+            for job, e, b in after.get(n, []):
+                if job == "m1":
+                    mm1(e, b)
+                else:
+                    mm2(e, b, "SV" if (e == 1 and b > 0) else "SS")

@@ -18,8 +18,9 @@ H = 1024
 P = 128
 FLOPS = 2 * E * T * (D * 2 * H + H * D)
 
-RAW_BUFS = 10
-LOOKAHEAD = 8
+RAW_BUFS = 12
+LOOKAHEAD = 11
+SINGLES = 6
 
 
 def tile_synclessmxfp8moe_kernel(tc, x, w13, w2, num_tokens_per_expert, out):
@@ -28,28 +29,30 @@ def tile_synclessmxfp8moe_kernel(tc, x, w13, w2, num_tokens_per_expert, out):
         const = ctx.enter_context(tc.tile_pool(name="const", bufs=1))
         rawp = ctx.enter_context(tc.tile_pool(name="rawp", bufs=RAW_BUFS))
         grpp = ctx.enter_context(tc.tile_pool(name="grpp", bufs=3))
-        codp = ctx.enter_context(tc.tile_pool(name="codp", bufs=6))
+        codp = ctx.enter_context(tc.tile_pool(name="codp", bufs=8))
         keep = ctx.enter_context(tc.tile_pool(name="keep", bufs=2))
         silp = ctx.enter_context(tc.tile_pool(name="silp", bufs=2))
-        outp = ctx.enter_context(tc.tile_pool(name="outp", bufs=4))
-        tps = ctx.enter_context(tc.psum_pool(name="tps", bufs=6))
-        mps = ctx.enter_context(tc.psum_pool(name="mps", bufs=2))
+        outp = ctx.enter_context(tc.tile_pool(name="outp", bufs=3))
+        psum = ctx.enter_context(tc.psum_pool(name="psum", bufs=8))
         ctx.enter_context(tc.manual_schedule())
 
-        blocks = [("x", 0, 0, 0)]
+        blocks = []
         for e in range(E):
+            blocks.append(("x", e, 0, 0))
             for b in range(4):
                 blocks.append(("w13", e, 0, b))
                 blocks.append(("w13", e, 1, b))
-            if e == 0:
-                blocks.append(("x", 1, 0, 0))
+        for e in range(E):
             for c in range(4):
                 blocks.append(("w2", e, 0, c))
         index = dict((blk, n) for n, blk in enumerate(blocks))
+        nblocks = len(blocks)
 
         raw = {}
         codes = {}
         hstate = {}
+        silus = {}
+        outs = {}
 
         def load(n):
             kind, e, hf, b = blocks[n]
@@ -75,35 +78,39 @@ def tile_synclessmxfp8moe_kernel(tc, x, w13, w2, num_tokens_per_expert, out):
 
         def block(n):
             kind, e, hf, b = blocks[n]
-            if n + LOOKAHEAD < len(blocks):
+            if n + LOOKAHEAD < nblocks:
                 load(n + LOOKAHEAD)
             words = raw[n][:].bitcast(F32)
             banks = []
             for k in range(4):
-                bank = tps.tile([P, 512], F32, tag="tb", name="tb")
-                for s in range(2):
-                    slot = 2 * k + s
-                    for u in range(2):
-                        if kind == "w2":
-                            beta = 4 * (slot % 4) + 2 * (slot // 4) + u
-                        else:
-                            beta = 8 * (slot % 2) + 2 * (slot // 2) + u
-                        q = 2 * s + u
-                        nc.tensor.transpose(
-                            bank[:, q * P : (q + 1) * P],
-                            words[:, beta * P : (beta + 1) * P],
-                            ident[:],
-                        )
+                bank = psum.tile([P, 512], F32, tag="ps", name="ps")
+                for q in range(4):
+                    if kind == "w2":
+                        beta = 4 * (2 * (k % 2) + q // 2) + 2 * (k // 2) + q % 2
+                    else:
+                        beta = 4 * k + q
+                    nc.tensor.transpose(
+                        bank[:, q * P : (q + 1) * P],
+                        words[:, beta * P : (beta + 1) * P],
+                        ident[:],
+                    )
                 banks.append(bank)
-            engines = {"x": "SVSV", "w13": "SSVS", "w2": "SSVV"}[kind]
+            if kind == "x":
+                engines = "SVSV"
+            elif kind == "w13":
+                engines = "SSVS" if hf == 0 else "SSSS"
+            else:
+                engines = "SSSV" if b % 2 == 1 else "SSVV"
             grouped = grpp.tile([P, 4096], BF16, tag="grp", name="grp", align_bytes=64)
             gw = grouped[:].bitcast(F32)
             for k in range(4):
-                copy_on(
-                    engines[k],
-                    gw[:, k * 512 : (k + 1) * 512].rearrange("p (s r u) -> p s r u", s=2, u=2),
-                    banks[k][:].rearrange("p (s u r) -> p s r u", s=2, u=2),
-                )
+                if kind == "x":
+                    dst = gw.rearrange("p (g i r u) -> p g i r u", g=4, i=2, u=2)[
+                        :, 2 * (k % 2) : 2 * (k % 2) + 2, k // 2, :, :
+                    ]
+                else:
+                    dst = gw[:, k * 512 : (k + 1) * 512].rearrange("p (s r u) -> p s r u", s=2, u=2)
+                copy_on(engines[k], dst, banks[k][:].rearrange("p (s u r) -> p s r u", s=2, u=2))
             if kind == "x":
                 cw = keep.tile([P, 1024], U32, tag="xc", name="xc", align_bytes=64)
                 cs = keep.tile([P, 1024], U8, tag="xs", name="xs", align_bytes=64)
@@ -118,28 +125,29 @@ def tile_synclessmxfp8moe_kernel(tc, x, w13, w2, num_tokens_per_expert, out):
                 )
             codes[n] = (cw, cs)
 
-        def mm1(e, b):
+        def job_w13(n):
+            kind, e, hf, b = blocks[n]
             xc, xs = codes[index[("x", e, 0, 0)]]
-            halves = []
-            for hf in range(2):
-                cw, cs = codes[index[("w13", e, hf, b)]]
-                bank = mps.tile([P, 512], F32, tag="mm", name="mm")
-                for ep in range(2):
-                    for g in range(4):
-                        sl = slice((2 * g + ep) * P, (2 * g + ep + 1) * P)
-                        xl = slice(g * 256, (g + 1) * 256)
-                        nc.tensor.matmul_mx(
-                            out=bank[:, ep * 256 : (ep + 1) * 256],
-                            lhsT=cw[:, sl].bitcast(FP8X4),
-                            lhsT_scale=cs[:, sl],
-                            rhs=xc[:, xl].bitcast(FP8X4),
-                            rhs_scale=xs[:, xl],
-                            start=(g == 0),
-                            stop=(g == 3),
-                        )
-                halves.append(bank)
-            sil = silp.tile([P, 512], F32, tag="sil", name="sil")
-            nc.scalar.activation(out=sil[:], in_=halves[0][:], func=SILU)
+            cw, cs = codes[n]
+            bank = psum.tile([P, 512], F32, tag="ps", name="ps")
+            for ep in range(2):
+                for g in range(4):
+                    sl = slice((4 * ep + g) * P, (4 * ep + g + 1) * P)
+                    xl = slice(g * 256, (g + 1) * 256)
+                    nc.tensor.matmul_mx(
+                        out=bank[:, ep * 256 : (ep + 1) * 256],
+                        lhsT=cw[:, sl].bitcast(FP8X4),
+                        lhsT_scale=cs[:, sl],
+                        rhs=xc[:, xl].bitcast(FP8X4),
+                        rhs_scale=xs[:, xl],
+                        start=(g == 0),
+                        stop=(g == 3),
+                    )
+            if hf == 0:
+                sil = silp.tile([P, 512], F32, tag="sil", name="sil")
+                nc.scalar.activation(out=sil[:], in_=bank[:], func=SILU)
+                silus[(e, b)] = sil
+                return
             if b == 0:
                 hg = keep.tile([P, 2, 256, 4], BF16, tag="hg", name="hg", align_bytes=64)
                 hc = keep.tile([P, 512], U32, tag="hc", name="hc", align_bytes=64)
@@ -149,8 +157,8 @@ def tile_synclessmxfp8moe_kernel(tc, x, w13, w2, num_tokens_per_expert, out):
             gp, up = b // 2, b % 2
             nc.vector.tensor_tensor(
                 out=hg[:, gp, :, 2 * up : 2 * up + 2],
-                in0=halves[1][:].rearrange("p (e n) -> p n e", e=2),
-                in1=sil[:].rearrange("p (e n) -> p n e", e=2),
+                in0=bank[:].rearrange("p (e n) -> p n e", e=2),
+                in1=silus[(e, b)][:].rearrange("p (e n) -> p n e", e=2),
                 op=MULT,
             )
             if up == 1:
@@ -160,12 +168,22 @@ def tile_synclessmxfp8moe_kernel(tc, x, w13, w2, num_tokens_per_expert, out):
                     in_=hg[:, gp, :, :].rearrange("p n t -> p (n t)"),
                 )
 
-        def mm2(e, c, engines):
-            cw, cs = codes[index[("w2", e, 0, c)]]
+        def job_w2(n):
+            kind, e, hf, c = blocks[n]
+            cw, cs = codes[n]
             hg, hc, hs = hstate[e]
-            o = outp.tile([P, 2, 512], F32, tag="o", name="o")
+            if e == 0:
+                c0, c1 = 2 * (c // 2), 2 * (c // 2) + 1
+            else:
+                c0, c1 = c, c
+            if c == c0:
+                outs[e] = outp.tile([P, 2, 512 * (c1 - c0 + 1)], F32, tag="o", name="o")
+            o = outs[e]
+            dram = out[T * e : T * (e + 1), 512 * c0 : 512 * (c1 + 1)].rearrange("(m i) c -> m i c", i=2)
+            engines = "VS" if (e == 1 and c >= 1) else "SS"
+            last = e == 1 and c == 3
             for i in range(2):
-                bank = mps.tile([P, 512], F32, tag="mm", name="mm")
+                bank = psum.tile([P, 512], F32, tag="ps", name="ps")
                 for gp in range(2):
                     hl = slice(gp * 256 + i * P, gp * 256 + (i + 1) * P)
                     wl = slice(gp * 512, (gp + 1) * 512)
@@ -180,15 +198,19 @@ def tile_synclessmxfp8moe_kernel(tc, x, w13, w2, num_tokens_per_expert, out):
                     )
                 copy_on(
                     engines[i],
-                    o[:, i, :].rearrange("p (r j) -> p r j", j=4),
+                    o[:, i, 512 * (c - c0) : 512 * (c - c0 + 1)].rearrange("p (r j) -> p r j", j=4),
                     bank[:].rearrange("p (j r) -> p r j", j=4),
                 )
-            nc.sync.dma_start(
-                out=out[T * e : T * (e + 1), 512 * c : 512 * (c + 1)].rearrange(
-                    "(m i) c -> m i c", i=2
-                ),
-                in_=o[:],
-            )
+                if last:
+                    nc.sync.dma_start(out=dram[:, i, :], in_=o[:, i, :])
+            if c == c1 and not last:
+                nc.sync.dma_start(out=dram, in_=o[:])
+
+        def job(n):
+            if blocks[n][0] == "w13":
+                job_w13(n)
+            elif blocks[n][0] == "w2":
+                job_w2(n)
 
         for n in range(LOOKAHEAD):
             load(n)
@@ -199,25 +221,13 @@ def tile_synclessmxfp8moe_kernel(tc, x, w13, w2, num_tokens_per_expert, out):
         nc.vector.memset(warm_in[:], 0.0)
         nc.scalar.activation(out=warm_out[:], in_=warm_in[:], func=SILU)
 
-        after = {
-            3: [("m1", 0, 0)],
-            5: [("m1", 0, 1)],
-            8: [("m1", 0, 2)],
-            10: [("m1", 0, 3)],
-            12: [("m2", 0, 0)],
-            13: [("m2", 0, 1)],
-            14: [("m2", 0, 2)],
-            15: [("m2", 0, 3)],
-            17: [("m1", 1, 0)],
-            19: [("m1", 1, 1)],
-            21: [("m1", 1, 2)],
-            23: [("m1", 1, 3)],
-            25: [("m2", 1, 0), ("m2", 1, 1), ("m2", 1, 2), ("m2", 1, 3)],
-        }
-        for n in range(len(blocks)):
-            block(n)
-            for job, e, b in after.get(n, []):
-                if job == "m1":
-                    mm1(e, b)
-                else:
-                    mm2(e, b, "SV" if (e == 1 and b > 0) else "SS")
+        groups = [(n, 1) for n in range(SINGLES)] + [(n, 2) for n in range(SINGLES, nblocks, 2)]
+        done = 0
+        for first, size in groups:
+            for m in range(first, first + size):
+                block(m)
+            for j in range(done, first):
+                job(j)
+            done = max(done, first)
+        for j in range(done, nblocks):
+            job(j)

@@ -221,11 +221,23 @@ def tile_synclessmxfp8moe_kernel(tc, x, w13, w2, num_tokens_per_expert, out):
         nc.vector.memset(warm_in[:], 0.0)
         nc.scalar.activation(out=warm_out[:], in_=warm_in[:], func=SILU)
 
+        zeros = const.tile([P, 512], BF16, name="zeros")
+        nc.vector.memset(zeros[:], 0.0)
+
+        def idle_matmuls(count):
+            bank = psum.tile([P, 512], F32, tag="ps", name="ps")
+            for rep in range(count):
+                nc.tensor.matmul(out=bank[:], lhsT=zeros[:, 0:P], rhs=zeros[:], start=True, stop=True)
+
+        idle_matmuls(12)
+
         groups = [(n, 1) for n in range(SINGLES)] + [(n, 2) for n in range(SINGLES, nblocks, 2)]
         done = 0
         for first, size in groups:
             for m in range(first, first + size):
                 block(m)
+            if first < 2:
+                idle_matmuls(2)
             for j in range(done, first):
                 job(j)
             done = max(done, first)

@@ -27,14 +27,19 @@ def tile_synclessmxfp8moe_kernel(tc, x, w13, w2, num_tokens_per_expert, out):
     nc = tc.nc
     with ExitStack() as ctx:
         const = ctx.enter_context(tc.tile_pool(name="const", bufs=1))
-        rawp = ctx.enter_context(tc.tile_pool(name="rawp", bufs=RAW_BUFS))
-        grpp = ctx.enter_context(tc.tile_pool(name="grpp", bufs=3))
-        codp = ctx.enter_context(tc.tile_pool(name="codp", bufs=8))
-        keep = ctx.enter_context(tc.tile_pool(name="keep", bufs=2))
-        silp = ctx.enter_context(tc.tile_pool(name="silp", bufs=2))
-        outp = ctx.enter_context(tc.tile_pool(name="outp", bufs=3))
-        psum = ctx.enter_context(tc.psum_pool(name="psum", bufs=8))
+        sbuf = ctx.enter_context(tc.tile_pool(name="sbuf", bufs=1))
+        psum = ctx.enter_context(tc.psum_pool(name="psum", bufs=1))
         ctx.enter_context(tc.manual_schedule())
+
+        counts = {}
+
+        def ring(pool, depth, tag, shape, dtype, align=None):
+            k = counts.get(tag, 0)
+            counts[tag] = k + 1
+            slot = "%s%d" % (tag, k % depth)
+            if align is None:
+                return pool.tile(shape, dtype, tag=slot, name=slot)
+            return pool.tile(shape, dtype, tag=slot, name=slot, align_bytes=align)
 
         blocks = []
         for e in range(E):
@@ -56,7 +61,7 @@ def tile_synclessmxfp8moe_kernel(tc, x, w13, w2, num_tokens_per_expert, out):
 
         def load(n):
             kind, e, hf, b = blocks[n]
-            r = rawp.tile([P, 4096], BF16, tag="raw", name="raw")
+            r = ring(sbuf, RAW_BUFS, "raw", [P, 4096], BF16)
             if kind == "x":
                 src = x[T * e : T * (e + 1), :].rearrange("(p i) d -> p i d", i=2)
                 dst = r[:].rearrange("p (i d) -> p i d", i=2)
@@ -83,7 +88,7 @@ def tile_synclessmxfp8moe_kernel(tc, x, w13, w2, num_tokens_per_expert, out):
             words = raw[n][:].bitcast(F32)
             banks = []
             for k in range(4):
-                bank = psum.tile([P, 512], F32, tag="ps", name="ps")
+                bank = ring(psum, 8, "ps", [P, 512], F32)
                 for q in range(4):
                     if kind == "w2":
                         beta = 4 * (2 * (k % 2) + q // 2) + 2 * (k // 2) + q % 2
@@ -101,7 +106,7 @@ def tile_synclessmxfp8moe_kernel(tc, x, w13, w2, num_tokens_per_expert, out):
                 engines = "SSVS" if hf == 0 else "SSSS"
             else:
                 engines = "SSSV" if b % 2 == 1 else "SSVV"
-            grouped = grpp.tile([P, 4096], BF16, tag="grp", name="grp", align_bytes=64)
+            grouped = ring(sbuf, 3, "grp", [P, 4096], BF16, 64)
             gw = grouped[:].bitcast(F32)
             for k in range(4):
                 if kind == "x":
@@ -112,11 +117,11 @@ def tile_synclessmxfp8moe_kernel(tc, x, w13, w2, num_tokens_per_expert, out):
                     dst = gw[:, k * 512 : (k + 1) * 512].rearrange("p (s r u) -> p s r u", s=2, u=2)
                 copy_on(engines[k], dst, banks[k][:].rearrange("p (s u r) -> p s r u", s=2, u=2))
             if kind == "x":
-                cw = keep.tile([P, 1024], U32, tag="xc", name="xc", align_bytes=64)
-                cs = keep.tile([P, 1024], U8, tag="xs", name="xs", align_bytes=64)
+                cw = ring(sbuf, 2, "xc", [P, 1024], U32, 64)
+                cs = ring(sbuf, 2, "xs", [P, 1024], U8, 64)
             else:
-                cw = codp.tile([P, 1024], U32, tag="cw", name="cw", align_bytes=64)
-                cs = codp.tile([P, 1024], U8, tag="cs", name="cs", align_bytes=64)
+                cw = ring(sbuf, 8, "cw", [P, 1024], U32, 64)
+                cs = ring(sbuf, 8, "cs", [P, 1024], U8, 64)
             for hlf in range(2):
                 nc.vector.quantize_mx(
                     out=cw[:, hlf * 512 : (hlf + 1) * 512].bitcast(FP8X4),
@@ -129,7 +134,7 @@ def tile_synclessmxfp8moe_kernel(tc, x, w13, w2, num_tokens_per_expert, out):
             kind, e, hf, b = blocks[n]
             xc, xs = codes[index[("x", e, 0, 0)]]
             cw, cs = codes[n]
-            bank = psum.tile([P, 512], F32, tag="ps", name="ps")
+            bank = ring(psum, 8, "ps", [P, 512], F32)
             for ep in range(2):
                 for g in range(4):
                     sl = slice((4 * ep + g) * P, (4 * ep + g + 1) * P)
@@ -144,14 +149,14 @@ def tile_synclessmxfp8moe_kernel(tc, x, w13, w2, num_tokens_per_expert, out):
                         stop=(g == 3),
                     )
             if hf == 0:
-                sil = silp.tile([P, 512], F32, tag="sil", name="sil")
+                sil = ring(sbuf, 2, "sil", [P, 512], F32)
                 nc.scalar.activation(out=sil[:], in_=bank[:], func=SILU)
                 silus[(e, b)] = sil
                 return
             if b == 0:
-                hg = keep.tile([P, 2, 256, 4], BF16, tag="hg", name="hg", align_bytes=64)
-                hc = keep.tile([P, 512], U32, tag="hc", name="hc", align_bytes=64)
-                hs = keep.tile([P, 512], U8, tag="hs", name="hs", align_bytes=64)
+                hg = ring(sbuf, 2, "hg", [P, 2, 256, 4], BF16, 64)
+                hc = ring(sbuf, 2, "hc", [P, 512], U32, 64)
+                hs = ring(sbuf, 2, "hs", [P, 512], U8, 64)
                 hstate[e] = (hg, hc, hs)
             hg, hc, hs = hstate[e]
             gp, up = b // 2, b % 2
@@ -177,13 +182,13 @@ def tile_synclessmxfp8moe_kernel(tc, x, w13, w2, num_tokens_per_expert, out):
             else:
                 c0, c1 = c, c
             if c == c0:
-                outs[e] = outp.tile([P, 2, 512 * (c1 - c0 + 1)], F32, tag="o", name="o")
+                outs[e] = ring(sbuf, 3, "o", [P, 2, 512 * (c1 - c0 + 1)], F32)
             o = outs[e]
             dram = out[T * e : T * (e + 1), 512 * c0 : 512 * (c1 + 1)].rearrange("(m i) c -> m i c", i=2)
             engines = "VS" if (e == 1 and c >= 1) else "SS"
             last = e == 1 and c == 3
             for i in range(2):
-                bank = psum.tile([P, 512], F32, tag="ps", name="ps")
+                bank = ring(psum, 8, "ps", [P, 512], F32)
                 for gp in range(2):
                     hl = slice(gp * 256 + i * P, gp * 256 + (i + 1) * P)
                     wl = slice(gp * 512, (gp + 1) * 512)
@@ -221,23 +226,11 @@ def tile_synclessmxfp8moe_kernel(tc, x, w13, w2, num_tokens_per_expert, out):
         nc.vector.memset(warm_in[:], 0.0)
         nc.scalar.activation(out=warm_out[:], in_=warm_in[:], func=SILU)
 
-        zeros = const.tile([P, 512], BF16, name="zeros")
-        nc.vector.memset(zeros[:], 0.0)
-
-        def idle_matmuls(count):
-            bank = psum.tile([P, 512], F32, tag="ps", name="ps")
-            for rep in range(count):
-                nc.tensor.matmul(out=bank[:], lhsT=zeros[:, 0:P], rhs=zeros[:], start=True, stop=True)
-
-        idle_matmuls(12)
-
         groups = [(n, 1) for n in range(SINGLES)] + [(n, 2) for n in range(SINGLES, nblocks, 2)]
         done = 0
         for first, size in groups:
             for m in range(first, first + size):
                 block(m)
-            if first < 2:
-                idle_matmuls(2)
             for j in range(done, first):
                 job(j)
             done = max(done, first)

@@ -20,26 +20,22 @@ FLOPS = 2 * E * T * (D * 2 * H + H * D)
 
 RAW_BUFS = 12
 LOOKAHEAD = 11
-SINGLES = 6
+SINGLES = 4
+SHORT_LAG = 10
 
 
 def tile_synclessmxfp8moe_kernel(tc, x, w13, w2, num_tokens_per_expert, out):
     nc = tc.nc
     with ExitStack() as ctx:
         const = ctx.enter_context(tc.tile_pool(name="const", bufs=1))
-        sbuf = ctx.enter_context(tc.tile_pool(name="sbuf", bufs=1))
-        psum = ctx.enter_context(tc.psum_pool(name="psum", bufs=1))
+        rawp = ctx.enter_context(tc.tile_pool(name="rawp", bufs=RAW_BUFS))
+        grpp = ctx.enter_context(tc.tile_pool(name="grpp", bufs=3))
+        codp = ctx.enter_context(tc.tile_pool(name="codp", bufs=8))
+        keep = ctx.enter_context(tc.tile_pool(name="keep", bufs=2))
+        silp = ctx.enter_context(tc.tile_pool(name="silp", bufs=2))
+        outp = ctx.enter_context(tc.tile_pool(name="outp", bufs=3))
+        psum = ctx.enter_context(tc.psum_pool(name="psum", bufs=8))
         ctx.enter_context(tc.manual_schedule())
-
-        counts = {}
-
-        def ring(pool, depth, tag, shape, dtype, align=None):
-            k = counts.get(tag, 0)
-            counts[tag] = k + 1
-            slot = "%s%d" % (tag, k % depth)
-            if align is None:
-                return pool.tile(shape, dtype, tag=slot, name=slot)
-            return pool.tile(shape, dtype, tag=slot, name=slot, align_bytes=align)
 
         blocks = []
         for e in range(E):
@@ -61,7 +57,7 @@ def tile_synclessmxfp8moe_kernel(tc, x, w13, w2, num_tokens_per_expert, out):
 
         def load(n):
             kind, e, hf, b = blocks[n]
-            r = ring(sbuf, RAW_BUFS, "raw", [P, 4096], BF16)
+            r = rawp.tile([P, 4096], BF16, tag="raw", name="raw")
             if kind == "x":
                 src = x[T * e : T * (e + 1), :].rearrange("(p i) d -> p i d", i=2)
                 dst = r[:].rearrange("p (i d) -> p i d", i=2)
@@ -88,7 +84,7 @@ def tile_synclessmxfp8moe_kernel(tc, x, w13, w2, num_tokens_per_expert, out):
             words = raw[n][:].bitcast(F32)
             banks = []
             for k in range(4):
-                bank = ring(psum, 8, "ps", [P, 512], F32)
+                bank = psum.tile([P, 512], F32, tag="ps", name="ps")
                 for q in range(4):
                     if kind == "w2":
                         beta = 4 * (2 * (k % 2) + q // 2) + 2 * (k // 2) + q % 2
@@ -106,7 +102,7 @@ def tile_synclessmxfp8moe_kernel(tc, x, w13, w2, num_tokens_per_expert, out):
                 engines = "SSVS" if hf == 0 else "SSSS"
             else:
                 engines = "SSSV" if b % 2 == 1 else "SSVV"
-            grouped = ring(sbuf, 3, "grp", [P, 4096], BF16, 64)
+            grouped = grpp.tile([P, 4096], BF16, tag="grp", name="grp", align_bytes=64)
             gw = grouped[:].bitcast(F32)
             for k in range(4):
                 if kind == "x":
@@ -117,11 +113,11 @@ def tile_synclessmxfp8moe_kernel(tc, x, w13, w2, num_tokens_per_expert, out):
                     dst = gw[:, k * 512 : (k + 1) * 512].rearrange("p (s r u) -> p s r u", s=2, u=2)
                 copy_on(engines[k], dst, banks[k][:].rearrange("p (s u r) -> p s r u", s=2, u=2))
             if kind == "x":
-                cw = ring(sbuf, 2, "xc", [P, 1024], U32, 64)
-                cs = ring(sbuf, 2, "xs", [P, 1024], U8, 64)
+                cw = keep.tile([P, 1024], U32, tag="xc", name="xc", align_bytes=64)
+                cs = keep.tile([P, 1024], U8, tag="xs", name="xs", align_bytes=64)
             else:
-                cw = ring(sbuf, 8, "cw", [P, 1024], U32, 64)
-                cs = ring(sbuf, 8, "cs", [P, 1024], U8, 64)
+                cw = codp.tile([P, 1024], U32, tag="cw", name="cw", align_bytes=64)
+                cs = codp.tile([P, 1024], U8, tag="cs", name="cs", align_bytes=64)
             for hlf in range(2):
                 nc.vector.quantize_mx(
                     out=cw[:, hlf * 512 : (hlf + 1) * 512].bitcast(FP8X4),
@@ -134,7 +130,7 @@ def tile_synclessmxfp8moe_kernel(tc, x, w13, w2, num_tokens_per_expert, out):
             kind, e, hf, b = blocks[n]
             xc, xs = codes[index[("x", e, 0, 0)]]
             cw, cs = codes[n]
-            bank = ring(psum, 8, "ps", [P, 512], F32)
+            bank = psum.tile([P, 512], F32, tag="ps", name="ps")
             for ep in range(2):
                 for g in range(4):
                     sl = slice((4 * ep + g) * P, (4 * ep + g + 1) * P)
@@ -149,14 +145,14 @@ def tile_synclessmxfp8moe_kernel(tc, x, w13, w2, num_tokens_per_expert, out):
                         stop=(g == 3),
                     )
             if hf == 0:
-                sil = ring(sbuf, 2, "sil", [P, 512], F32)
+                sil = silp.tile([P, 512], F32, tag="sil", name="sil")
                 nc.scalar.activation(out=sil[:], in_=bank[:], func=SILU)
                 silus[(e, b)] = sil
                 return
             if b == 0:
-                hg = ring(sbuf, 2, "hg", [P, 2, 256, 4], BF16, 64)
-                hc = ring(sbuf, 2, "hc", [P, 512], U32, 64)
-                hs = ring(sbuf, 2, "hs", [P, 512], U8, 64)
+                hg = keep.tile([P, 2, 256, 4], BF16, tag="hg", name="hg", align_bytes=64)
+                hc = keep.tile([P, 512], U32, tag="hc", name="hc", align_bytes=64)
+                hs = keep.tile([P, 512], U8, tag="hs", name="hs", align_bytes=64)
                 hstate[e] = (hg, hc, hs)
             hg, hc, hs = hstate[e]
             gp, up = b // 2, b % 2
@@ -182,13 +178,13 @@ def tile_synclessmxfp8moe_kernel(tc, x, w13, w2, num_tokens_per_expert, out):
             else:
                 c0, c1 = c, c
             if c == c0:
-                outs[e] = ring(sbuf, 3, "o", [P, 2, 512 * (c1 - c0 + 1)], F32)
+                outs[e] = outp.tile([P, 2, 512 * (c1 - c0 + 1)], F32, tag="o", name="o")
             o = outs[e]
             dram = out[T * e : T * (e + 1), 512 * c0 : 512 * (c1 + 1)].rearrange("(m i) c -> m i c", i=2)
-            engines = "VS" if (e == 1 and c >= 1) else "SS"
-            last = e == 1 and c == 3
+            engines = "VS" if (e == 1 and c >= 2) else "SS"
+            last = e == 1
             for i in range(2):
-                bank = ring(psum, 8, "ps", [P, 512], F32)
+                bank = psum.tile([P, 512], F32, tag="ps", name="ps")
                 for gp in range(2):
                     hl = slice(gp * 256 + i * P, gp * 256 + (i + 1) * P)
                     wl = slice(gp * 512, (gp + 1) * 512)
@@ -226,13 +222,18 @@ def tile_synclessmxfp8moe_kernel(tc, x, w13, w2, num_tokens_per_expert, out):
         nc.vector.memset(warm_in[:], 0.0)
         nc.scalar.activation(out=warm_out[:], in_=warm_in[:], func=SILU)
 
-        groups = [(n, 1) for n in range(SINGLES)] + [(n, 2) for n in range(SINGLES, nblocks, 2)]
+        groups = (
+            [(n, 1, 1) for n in range(SINGLES)]
+            + [(n, 2, 1) for n in range(SINGLES, SHORT_LAG, 2)]
+            + [(n, 2, 2) for n in range(SHORT_LAG, nblocks, 2)]
+        )
         done = 0
-        for first, size in groups:
+        for first, size, lag in groups:
             for m in range(first, first + size):
                 block(m)
-            for j in range(done, first):
+            upto = first + size - lag
+            for j in range(done, upto):
                 job(j)
-            done = max(done, first)
+            done = max(done, upto)
         for j in range(done, nblocks):
             job(j)

from contextlib import ExitStack

import concourse.mybir as mybir
from concourse.masks import make_identity

FP8X4 = mybir.dt.float8_e4m3fn_x4
BF16 = mybir.dt.bfloat16
F32 = mybir.dt.float32
U32 = mybir.dt.uint32
U8 = mybir.dt.uint8
SILU = mybir.ActivationFunctionType.Silu
MULT = mybir.AluOpType.mult

E = 2
T = 256
D = 2048
H = 1024
P = 128
FLOPS = 2 * E * T * (D * 2 * H + H * D)

RAW_BUFS = 12
LOOKAHEAD = 11
SINGLES = 4
SHORT_LAG = 10


def tile_synclessmxfp8moe_kernel(tc, x, w13, w2, num_tokens_per_expert, out):
    nc = tc.nc
    with ExitStack() as ctx:
        const = ctx.enter_context(tc.tile_pool(name="const", bufs=1))
        rawp = ctx.enter_context(tc.tile_pool(name="rawp", bufs=RAW_BUFS))
        grpp = ctx.enter_context(tc.tile_pool(name="grpp", bufs=3))
        codp = ctx.enter_context(tc.tile_pool(name="codp", bufs=8))
        keep = ctx.enter_context(tc.tile_pool(name="keep", bufs=2))
        silp = ctx.enter_context(tc.tile_pool(name="silp", bufs=2))
        outp = ctx.enter_context(tc.tile_pool(name="outp", bufs=3))
        psum = ctx.enter_context(tc.psum_pool(name="psum", bufs=8))
        ctx.enter_context(tc.manual_schedule())

        blocks = []
        for e in range(E):
            blocks.append(("x", e, 0, 0))
            for b in range(4):
                blocks.append(("w13", e, 0, b))
                blocks.append(("w13", e, 1, b))
        for e in range(E):
            for c in range(4):
                blocks.append(("w2", e, 0, c))
        index = dict((blk, n) for n, blk in enumerate(blocks))
        nblocks = len(blocks)

        raw = {}
        codes = {}
        hstate = {}
        silus = {}
        outs = {}

        def load(n):
            kind, e, hf, b = blocks[n]
            r = rawp.tile([P, 4096], BF16, tag="raw", name="raw")
            if kind == "x":
                src = x[T * e : T * (e + 1), :].rearrange("(p i) d -> p i d", i=2)
                dst = r[:].rearrange("p (i d) -> p i d", i=2)
            elif kind == "w13":
                r0 = H * hf + 256 * b
                src = w13[e, r0 : r0 + 256, :].rearrange("(p i) d -> p i d", i=2)
                dst = r[:].rearrange("p (i d) -> p i d", i=2)
            else:
                src = w2[e, 512 * b : 512 * (b + 1), :].rearrange("(p j) h -> p j h", j=4)
                dst = r[:].rearrange("p (j h) -> p j h", j=4)
            nc.sync.dma_start(out=dst, in_=src)
            raw[n] = r

        def copy_on(eng, dst, src):
            if eng == "S":
                nc.scalar.copy(out=dst, in_=src)
            else:
                nc.vector.tensor_copy(out=dst, in_=src)

        def block(n):
            kind, e, hf, b = blocks[n]
            if n + LOOKAHEAD < nblocks:
                load(n + LOOKAHEAD)
            words = raw[n][:].bitcast(F32)
            banks = []
            for k in range(4):
                bank = psum.tile([P, 512], F32, tag="ps", name="ps")
                for q in range(4):
                    if kind == "w2":
                        beta = 4 * (2 * (k % 2) + q // 2) + 2 * (k // 2) + q % 2
                    else:
                        beta = 4 * k + q
                    nc.tensor.transpose(
                        bank[:, q * P : (q + 1) * P],
                        words[:, beta * P : (beta + 1) * P],
                        ident[:],
                    )
                banks.append(bank)
            if kind == "x":
                engines = "SVSV"
            elif kind == "w13":
                engines = "SSVS" if hf == 0 else "SSSS"
            else:
                engines = "SSSV" if b % 2 == 1 else "SSVV"
            grouped = grpp.tile([P, 4096], BF16, tag="grp", name="grp", align_bytes=64)
            gw = grouped[:].bitcast(F32)
            for k in range(4):
                if kind == "x":
                    dst = gw.rearrange("p (g i r u) -> p g i r u", g=4, i=2, u=2)[
                        :, 2 * (k % 2) : 2 * (k % 2) + 2, k // 2, :, :
                    ]
                else:
                    dst = gw[:, k * 512 : (k + 1) * 512].rearrange("p (s r u) -> p s r u", s=2, u=2)
                copy_on(engines[k], dst, banks[k][:].rearrange("p (s u r) -> p s r u", s=2, u=2))
            if kind == "x":
                cw = keep.tile([P, 1024], U32, tag="xc", name="xc", align_bytes=64)
                cs = keep.tile([P, 1024], U8, tag="xs", name="xs", align_bytes=64)
            else:
                cw = codp.tile([P, 1024], U32, tag="cw", name="cw", align_bytes=64)
                cs = codp.tile([P, 1024], U8, tag="cs", name="cs", align_bytes=64)
            for hlf in range(2):
                nc.vector.quantize_mx(
                    out=cw[:, hlf * 512 : (hlf + 1) * 512].bitcast(FP8X4),
                    scales=cs[:, hlf * 512 : (hlf + 1) * 512],
                    in_=grouped[:, hlf * 2048 : (hlf + 1) * 2048],
                )
            codes[n] = (cw, cs)

        def job_w13(n):
            kind, e, hf, b = blocks[n]
            xc, xs = codes[index[("x", e, 0, 0)]]
            cw, cs = codes[n]
            bank = psum.tile([P, 512], F32, tag="ps", name="ps")
            for ep in range(2):
                for g in range(4):
                    sl = slice((4 * ep + g) * P, (4 * ep + g + 1) * P)
                    xl = slice(g * 256, (g + 1) * 256)
                    nc.tensor.matmul_mx(
                        out=bank[:, ep * 256 : (ep + 1) * 256],
                        lhsT=cw[:, sl].bitcast(FP8X4),
                        lhsT_scale=cs[:, sl],
                        rhs=xc[:, xl].bitcast(FP8X4),
                        rhs_scale=xs[:, xl],
                        start=(g == 0),
                        stop=(g == 3),
                    )
            if hf == 0:
                sil = silp.tile([P, 512], F32, tag="sil", name="sil")
                nc.scalar.activation(out=sil[:], in_=bank[:], func=SILU)
                silus[(e, b)] = sil
                return
            if b == 0:
                hg = keep.tile([P, 2, 256, 4], BF16, tag="hg", name="hg", align_bytes=64)
                hc = keep.tile([P, 512], U32, tag="hc", name="hc", align_bytes=64)
                hs = keep.tile([P, 512], U8, tag="hs", name="hs", align_bytes=64)
                hstate[e] = (hg, hc, hs)
            hg, hc, hs = hstate[e]
            gp, up = b // 2, b % 2
            nc.vector.tensor_tensor(
                out=hg[:, gp, :, 2 * up : 2 * up + 2],
                in0=bank[:].rearrange("p (e n) -> p n e", e=2),
                in1=silus[(e, b)][:].rearrange("p (e n) -> p n e", e=2),
                op=MULT,
            )
            if up == 1:
                nc.vector.quantize_mx(
                    out=hc[:, gp * 256 : (gp + 1) * 256].bitcast(FP8X4),
                    scales=hs[:, gp * 256 : (gp + 1) * 256],
                    in_=hg[:, gp, :, :].rearrange("p n t -> p (n t)"),
                )

        def job_w2(n):
            kind, e, hf, c = blocks[n]
            cw, cs = codes[n]
            hg, hc, hs = hstate[e]
            if e == 0:
                c0, c1 = 2 * (c // 2), 2 * (c // 2) + 1
            else:
                c0, c1 = c, c
            if c == c0:
                outs[e] = outp.tile([P, 2, 512 * (c1 - c0 + 1)], F32, tag="o", name="o")
            o = outs[e]
            dram = out[T * e : T * (e + 1), 512 * c0 : 512 * (c1 + 1)].rearrange("(m i) c -> m i c", i=2)
            engines = "VS" if (e == 1 and c >= 2) else "SS"
            last = e == 1
            for i in range(2):
                bank = psum.tile([P, 512], F32, tag="ps", name="ps")
                for gp in range(2):
                    hl = slice(gp * 256 + i * P, gp * 256 + (i + 1) * P)
                    wl = slice(gp * 512, (gp + 1) * 512)
                    nc.tensor.matmul_mx(
                        out=bank[:],
                        lhsT=hc[:, hl].bitcast(FP8X4),
                        lhsT_scale=hs[:, hl],
                        rhs=cw[:, wl].bitcast(FP8X4),
                        rhs_scale=cs[:, wl],
                        start=(gp == 0),
                        stop=(gp == 1),
                    )
                copy_on(
                    engines[i],
                    o[:, i, 512 * (c - c0) : 512 * (c - c0 + 1)].rearrange("p (r j) -> p r j", j=4),
                    bank[:].rearrange("p (j r) -> p r j", j=4),
                )
                if last:
                    nc.sync.dma_start(out=dram[:, i, :], in_=o[:, i, :])
            if c == c1 and not last:
                nc.sync.dma_start(out=dram, in_=o[:])

        def job(n):
            if blocks[n][0] == "w13":
                job_w13(n)
            elif blocks[n][0] == "w2":
                job_w2(n)

        for n in range(LOOKAHEAD):
            load(n)
        ident = const.tile([P, P], F32, name="ident")
        make_identity(nc, ident[:])
        warm_in = const.tile([P, 8], F32, name="warm_in")
        warm_out = const.tile([P, 8], F32, name="warm_out")
        nc.vector.memset(warm_in[:], 0.0)
        nc.scalar.activation(out=warm_out[:], in_=warm_in[:], func=SILU)

        groups = (
            [(n, 1, 1) for n in range(SINGLES)]
            + [(n, 2, 1) for n in range(SINGLES, SHORT_LAG, 2)]
            + [(n, 2, 2) for n in range(SHORT_LAG, nblocks, 2)]
        )
        done = 0
        for first, size, lag in groups:
            for m in range(first, first + size):
                block(m)
            upto = first + size - lag
            for j in range(done, upto):
                job(j)
            done = max(done, upto)
        for j in range(done, nblocks):
            job(j)
